import numpy as np
import ml_dtypes


def mxq(x, axis, fmt="e4m3"):
    dtype, down = {"e4m3": (ml_dtypes.float8_e4m3fn, 7), "e5m2": (ml_dtypes.float8_e5m2, 14)}[fmt]
    v = np.moveaxis(np.asarray(x, np.float32).astype(ml_dtypes.bfloat16).astype(np.float64), axis, -1)
    blocks = v.reshape(v.shape[:-1] + (-1, 32))
    amax = np.abs(blocks).max(-1, keepdims=True)
    byte = np.maximum(np.where(amax > 0, np.frexp(amax)[1] - 1 + 127, 0) - down, 1)
    scale = np.exp2(byte - 127.0)
    codes = (blocks / scale).astype(np.float32).astype(dtype).astype(np.float64)
    return np.moveaxis((codes * scale).reshape(v.shape), -1, axis)


WIDE = False


def mx_kscale(k):
    if not WIDE:
        return np.ones(k)
    levels = np.array([30, -30])
    if k % 512:
        return np.exp2(np.random.permutation(np.resize(levels, k // 32))).repeat(32)
    a = np.empty((k // 512, 16))
    for p in range(k // 512):
        a[p, :8] = np.random.permutation(np.resize(levels, 8))
        for g in range(8):
            far = levels[np.abs(levels - a[p, g]) >= 10]
            a[p, g + 8] = far[np.random.randint(len(far))]
    return np.exp2(a.ravel()).repeat(32)


BF16 = ml_dtypes.bfloat16


def bf(x):
    return np.asarray(x, np.float32).astype(BF16)


def f64(x):
    return np.asarray(x).astype(np.float64)


B, K, N = 16384, 512, 256


def setup_inputs():
    s = mx_kscale(K)
    return {"x": bf(np.random.standard_normal((B, K)) * s),
            "dft_real": bf(np.random.standard_normal((N, K)) / np.sqrt(K) / s[None, :]),
            "dft_imag": bf(np.random.standard_normal((N, K)) / np.sqrt(K) / s[None, :])}


def reference(x, dft_real, dft_imag):
    xq = mxq(f64(x), 1, "e5m2")
    rxs = xq @ mxq(f64(dft_real), 1, "e4m3").T
    ixs = xq @ mxq(f64(dft_imag), 1, "e4m3").T
    mag = np.log(rxs * rxs + ixs * ixs)
    return mag

@@ -1,0 +1,184 @@
+from contextlib import ExitStack
+
+import concourse.mybir as mybir
+from concourse.masks import make_identity
+
+B, K, N = 16384, 512, 256
+FLOPS = 2 * B * K * 2 * N
+
+F32 = mybir.dt.float32
+BF16 = mybir.dt.bfloat16
+U32 = mybir.dt.uint32
+U8 = mybir.dt.uint8
+E4M3X4 = mybir.dt.float8_e4m3fn_x4
+E5M2X4 = mybir.dt.float8_e5m2_x4
+ACT = mybir.ActivationFunctionType
+ALU = mybir.AluOpType
+
+P = 128
+TILES = 4
+WORDS = K // 2
+SIZES = [2, 2] + [4] * 31
+GROUPS = len(SIZES)
+LOAD_AHEAD = 4
+HEAD_GROUPS = 1
+VECTOR_ADD_GROUPS = 1
+assert sum(SIZES) * P == B
+
+
+def tile_dft_kernel(tc, x, dft_real, dft_imag, out):
+    nc = tc.nc
+    first_row = [sum(SIZES[:g]) * P for g in range(GROUPS + 1)]
+
+    def vector_tiles(g):
+        if g < HEAD_GROUPS:
+            return []
+        return [1]
+
+    with ExitStack() as ctx:
+        keep = ctx.enter_context(tc.tile_pool(name="keep", bufs=1))
+        raw_pool = ctx.enter_context(tc.tile_pool(name="raw", bufs=LOAD_AHEAD + 2))
+        kt_pool = ctx.enter_context(tc.tile_pool(name="kt", bufs=3))
+        code_pool = ctx.enter_context(tc.tile_pool(name="code", bufs=3))
+        sq_pool = ctx.enter_context(tc.tile_pool(name="sq", bufs=3))
+        tmp_pool = ctx.enter_context(tc.tile_pool(name="tmp", bufs=2))
+        pow_pool = ctx.enter_context(tc.tile_pool(name="pow", bufs=3))
+        out_pool = ctx.enter_context(tc.tile_pool(name="res", bufs=4))
+        t_psum = ctx.enter_context(tc.psum_pool(name="t_psum", bufs=2))
+        m_psum = ctx.enter_context(tc.psum_pool(name="m_psum", bufs=6))
+        ctx.enter_context(tc.manual_schedule())
+
+        ident = keep.tile([P, P], F32, name="ident")
+        make_identity(nc, ident[:])
+        w_raw = keep.tile([P, TILES, K], BF16, name="w_raw")
+        w_codes = keep.tile([P, 2 * N], U32, name="w_codes", align_bytes=64)
+        w_scales = keep.tile([P, 2 * N], U8, name="w_scales", align_bytes=64)
+
+        raw, t_banks, kt, codes, scales, m_banks, sq, power = {}, {}, {}, {}, {}, {}, {}, {}
+
+        def load(g):
+            n = SIZES[g]
+            raw[g] = raw_pool.tile([P, TILES, K], BF16, name="x_raw")
+            rows = x[first_row[g] : first_row[g + 1], :]
+            nc.sync.dma_start(out=raw[g][:, :n, :], in_=rows.rearrange("(p j) k -> p j k", j=n))
+
+        def transpose(g, src, n):
+            words = src[:].rearrange("p j k -> p (j k)").bitcast(F32)
+            t_banks[g] = []
+            for half in range(n // 2):
+                bank = t_psum.tile([P, 2, 2, P], F32, name="t_bank")
+                for jj in range(2):
+                    w0 = (2 * half + jj) * WORDS
+                    for u in range(2):
+                        nc.tensor.transpose(bank[:, jj, u, :], words[:, w0 + u : w0 + WORDS : 2], ident[:])
+                t_banks[g].append(bank)
+            kt[g] = kt_pool.tile([P, TILES * K], BF16, name="kt", align_bytes=64)
+
+        def interleave(g, half, on_scalar):
+            dst = kt[g][:].bitcast(F32)[:, half * K : (half + 1) * K].rearrange("p (j r u) -> p j r u", j=2, u=2)
+            src = t_banks[g][half][:].rearrange("p j u r -> p j r u")
+            if on_scalar:
+                nc.scalar.copy(out=dst, in_=src)
+            else:
+                nc.vector.tensor_copy(out=dst, in_=src)
+
+        def quantize(g):
+            n = SIZES[g]
+            codes[g] = code_pool.tile([P, TILES * P], U32, name="x_codes", align_bytes=64)
+            scales[g] = code_pool.tile([P, TILES * P], U8, name="x_scales", align_bytes=64)
+            nc.vector.quantize_mx(
+                out=codes[g][:, : n * P].bitcast(E5M2X4), scales=scales[g][:, : n * P], in_=kt[g][:, : n * K]
+            )
+
+        def quantize_weights(half):
+            cols = slice(half * N, (half + 1) * N)
+            nc.vector.quantize_mx(
+                out=w_codes[:, cols].bitcast(E4M3X4),
+                scales=w_scales[:, cols],
+                in_=kt["w"][:, half * 2 * K : (half + 1) * 2 * K],
+            )
+
+        def multiply(g):
+            m_banks[g] = []
+            for j in range(SIZES[g]):
+                bank = m_psum.tile([P, 2, N], F32, name="m_bank")
+                cols = slice(j * P, (j + 1) * P)
+                nc.tensor.matmul_mx(
+                    out=bank[:].rearrange("p c n -> p (c n)"),
+                    lhsT=codes[g][:, cols].bitcast(E5M2X4),
+                    lhsT_scale=scales[g][:, cols],
+                    rhs=w_codes[:].bitcast(E4M3X4),
+                    rhs_scale=w_scales[:],
+                    start=True,
+                    stop=True,
+                )
+                m_banks[g].append(bank)
+            sq[g] = sq_pool.tile([P, 2, TILES, N], F32, name="sq")
+
+        def square_on_scalar(g, j):
+            nc.scalar.activation(out=sq[g][:, :, j, :], in_=m_banks[g][j][:], func=ACT.Square)
+
+        def square_on_vector(g, j):
+            held = tmp_pool.tile([P, 2, N], F32, name="held")
+            for c in range(2):
+                nc.vector.tensor_copy(out=held[:, c, :], in_=m_banks[g][j][:, c, :])
+            for c in range(2):
+                nc.vector.tensor_tensor(
+                    out=sq[g][:, c, j, :], in0=m_banks[g][j][:, c, :], in1=held[:, c, :], op=ALU.mult
+                )
+
+        def add(g):
+            n = SIZES[g]
+            power[g] = pow_pool.tile([P, TILES, N], F32, name="power")
+            engine = nc.gpsimd if g < GROUPS - VECTOR_ADD_GROUPS else nc.vector
+            engine.tensor_tensor(
+                out=power[g][:, :n, :].rearrange("p j n -> p (j n)"),
+                in0=sq[g][:, 0, :n, :].rearrange("p j n -> p (j n)"),
+                in1=sq[g][:, 1, :n, :].rearrange("p j n -> p (j n)"),
+                op=ALU.add,
+            )
+
+        def log_and_store(g):
+            n = SIZES[g]
+            res = out_pool.tile([P, TILES, N], F32, name="res")
+            nc.scalar.activation(out=res[:, :n, :], in_=power[g][:, :n, :], func=ACT.Ln)
+            rows = out[first_row[g] : first_row[g + 1], :]
+            nc.sync.dma_start(out=rows.rearrange("(p j) n -> p j n", j=n), in_=res[:, :n, :])
+
+        nc.sync.dma_start(out=w_raw[:, 0:2, :], in_=dft_real.rearrange("(j p) k -> p j k", p=P))
+        nc.sync.dma_start(out=w_raw[:, 2:4, :], in_=dft_imag.rearrange("(j p) k -> p j k", p=P))
+        for g in range(LOAD_AHEAD):
+            load(g)
+
+        transpose("w", w_raw, TILES)
+        interleave("w", 0, True)
+        interleave("w", 1, False)
+        transpose(0, raw[0], SIZES[0])
+        for half in range(SIZES[0] // 2):
+            interleave(0, half, True)
+        quantize_weights(0)
+        quantize_weights(1)
+
+        for s in range(GROUPS + 2):
+            if s + LOAD_AHEAD < GROUPS:
+                load(s + LOAD_AHEAD)
+            if s + 1 < GROUPS:
+                transpose(s + 1, raw[s + 1], SIZES[s + 1])
+            if s < GROUPS:
+                quantize(s)
+            if 0 <= s - 1 < GROUPS:
+                add(s - 1)
+            if s < GROUPS:
+                multiply(s)
+            if s + 1 < GROUPS:
+                for half in range(SIZES[s + 1] // 2):
+                    interleave(s + 1, half, False)
+            if s < GROUPS:
+                for j in vector_tiles(s):
+                    square_on_vector(s, j)
+            if 0 <= s - 2 < GROUPS:
+                log_and_store(s - 2)
+            if s < GROUPS:
+                for j in range(SIZES[s]):
+                    if j not in vector_tiles(s):
+                        square_on_scalar(s, j)

@@ -16,13 +16,24 @@ ACT = mybir.ActivationFunctionType
 ALU = mybir.AluOpType
 
 P = 128
-TILES = 4
+TILES = 8
+RUN = 4
 WORDS = K // 2
-SIZES = [2, 2] + [4] * 31
+SIZES = [2, 2, 4] + [8] * 15
 GROUPS = len(SIZES)
-LOAD_AHEAD = 4
-HEAD_GROUPS = 1
-VECTOR_ADD_GROUPS = 1
+LOAD_AHEAD = 3
+HEAD_GROUPS = 3
+HEAD_COPY_GROUPS = 0
+VECTOR_ADD_GROUPS = 0
+VECTOR_ADD_COLS = 256
+HALF_HEAD_GROUPS = 5
+LAST_VECTOR_TILES = (1, 3, 5)
+LAST_ADD_COLS = 768
+LAST_PIECES = 2
+SHARED_COLS = 192
+T_BANKS = 2
+M_BANKS = 6
+FIRST_RUN = 5
 assert sum(SIZES) * P == B
 
 
@@ -30,31 +41,41 @@ def tile_dft_kernel(tc, x, dft_real, dft_imag, out):
     nc = tc.nc
     first_row = [sum(SIZES[:g]) * P for g in range(GROUPS + 1)]
 
-    def vector_tiles(g):
+    def vector_share(g, j):
         if g < HEAD_GROUPS:
-            return []
-        return [1]
+            return 0
+        if g == GROUPS - 1:
+            return N if j in LAST_VECTOR_TILES else 0
+        if j == 1:
+            return N
+        if g < HALF_HEAD_GROUPS:
+            return 0
+        if j == 4 and SIZES[g] == TILES:
+            return SHARED_COLS
+        return 0
 
     with ExitStack() as ctx:
         keep = ctx.enter_context(tc.tile_pool(name="keep", bufs=1))
         raw_pool = ctx.enter_context(tc.tile_pool(name="raw", bufs=LOAD_AHEAD + 2))
-        kt_pool = ctx.enter_context(tc.tile_pool(name="kt", bufs=3))
-        code_pool = ctx.enter_context(tc.tile_pool(name="code", bufs=3))
+        kt_pool = ctx.enter_context(tc.tile_pool(name="kt", bufs=4))
+        code_pool = ctx.enter_context(tc.tile_pool(name="code", bufs=2))
         sq_pool = ctx.enter_context(tc.tile_pool(name="sq", bufs=3))
         tmp_pool = ctx.enter_context(tc.tile_pool(name="tmp", bufs=2))
-        pow_pool = ctx.enter_context(tc.tile_pool(name="pow", bufs=3))
         out_pool = ctx.enter_context(tc.tile_pool(name="res", bufs=4))
-        t_psum = ctx.enter_context(tc.psum_pool(name="t_psum", bufs=2))
-        m_psum = ctx.enter_context(tc.psum_pool(name="m_psum", bufs=6))
+        t_psum = ctx.enter_context(tc.psum_pool(name="t_psum", bufs=T_BANKS))
+        m_psum = ctx.enter_context(tc.psum_pool(name="m_psum", bufs=M_BANKS))
         ctx.enter_context(tc.manual_schedule())
 
         ident = keep.tile([P, P], F32, name="ident")
         make_identity(nc, ident[:])
-        w_raw = keep.tile([P, TILES, K], BF16, name="w_raw")
+        w_raw = keep.tile([P, RUN, K], BF16, name="w_raw")
         w_codes = keep.tile([P, 2 * N], U32, name="w_codes", align_bytes=64)
         w_scales = keep.tile([P, 2 * N], U8, name="w_scales", align_bytes=64)
 
-        raw, t_banks, kt, codes, scales, m_banks, sq, power = {}, {}, {}, {}, {}, {}, {}, {}
+        raw, t_banks, kt, codes, scales, m_banks, sq, power, held = {}, {}, {}, {}, {}, {}, {}, {}, {}
+
+        def new_kt():
+            return kt_pool.tile([P, TILES * WORDS + LAST_ADD_COLS], F32, name="kt", align_bytes=64)
 
         def load(g):
             n = SIZES[g]
@@ -62,21 +83,19 @@ def tile_dft_kernel(tc, x, dft_real, dft_imag, out):
             rows = x[first_row[g] : first_row[g + 1], :]
             nc.sync.dma_start(out=raw[g][:, :n, :], in_=rows.rearrange("(p j) k -> p j k", j=n))
 
-        def transpose(g, src, n):
+        def transpose(g, src, pairs):
             words = src[:].rearrange("p j k -> p (j k)").bitcast(F32)
-            t_banks[g] = []
-            for half in range(n // 2):
+            for pair in pairs:
                 bank = t_psum.tile([P, 2, 2, P], F32, name="t_bank")
                 for jj in range(2):
-                    w0 = (2 * half + jj) * WORDS
+                    w0 = (2 * pair + jj) * WORDS
                     for u in range(2):
                         nc.tensor.transpose(bank[:, jj, u, :], words[:, w0 + u : w0 + WORDS : 2], ident[:])
-                t_banks[g].append(bank)
-            kt[g] = kt_pool.tile([P, TILES * K], BF16, name="kt", align_bytes=64)
+                t_banks[g, pair] = bank
 
-        def interleave(g, half, on_scalar):
-            dst = kt[g][:].bitcast(F32)[:, half * K : (half + 1) * K].rearrange("p (j r u) -> p j r u", j=2, u=2)
-            src = t_banks[g][half][:].rearrange("p j u r -> p j r u")
+        def interleave(g, pair, on_scalar):
+            dst = kt[g][:, pair * K : (pair + 1) * K].rearrange("p (j r u) -> p j r u", j=2, u=2)
+            src = t_banks[g, pair][:].rearrange("p j u r -> p j r u")
             if on_scalar:
                 nc.scalar.copy(out=dst, in_=src)
             else:
@@ -87,7 +106,9 @@ def tile_dft_kernel(tc, x, dft_real, dft_imag, out):
             codes[g] = code_pool.tile([P, TILES * P], U32, name="x_codes", align_bytes=64)
             scales[g] = code_pool.tile([P, TILES * P], U8, name="x_scales", align_bytes=64)
             nc.vector.quantize_mx(
-                out=codes[g][:, : n * P].bitcast(E5M2X4), scales=scales[g][:, : n * P], in_=kt[g][:, : n * K]
+                out=codes[g][:, : n * P].bitcast(E5M2X4),
+                scales=scales[g][:, : n * P],
+                in_=kt[g][:, : n * WORDS].bitcast(BF16),
             )
 
         def quantize_weights(half):
@@ -95,12 +116,11 @@ def tile_dft_kernel(tc, x, dft_real, dft_imag, out):
             nc.vector.quantize_mx(
                 out=w_codes[:, cols].bitcast(E4M3X4),
                 scales=w_scales[:, cols],
-                in_=kt["w"][:, half * 2 * K : (half + 1) * 2 * K],
+                in_=kt["w"][:, half * K : (half + 1) * K].bitcast(BF16),
             )
 
-        def multiply(g):
-            m_banks[g] = []
-            for j in range(SIZES[g]):
+        def multiply(g, tiles):
+            for j in tiles:
                 bank = m_psum.tile([P, 2, N], F32, name="m_bank")
                 cols = slice(j * P, (j + 1) * P)
                 nc.tensor.matmul_mx(
@@ -112,73 +132,99 @@ def tile_dft_kernel(tc, x, dft_real, dft_imag, out):
                     start=True,
                     stop=True,
                 )
-                m_banks[g].append(bank)
-            sq[g] = sq_pool.tile([P, 2, TILES, N], F32, name="sq")
+                m_banks[g, j] = bank
 
         def square_on_scalar(g, j):
-            nc.scalar.activation(out=sq[g][:, :, j, :], in_=m_banks[g][j][:], func=ACT.Square)
+            c0 = vector_share(g, j)
+            if c0 < N:
+                nc.scalar.activation(out=sq[g][:, :, j, c0:], in_=m_banks[g, j][:, :, c0:], func=ACT.Square)
 
         def square_on_vector(g, j):
-            held = tmp_pool.tile([P, 2, N], F32, name="held")
-            for c in range(2):
-                nc.vector.tensor_copy(out=held[:, c, :], in_=m_banks[g][j][:, c, :])
-            for c in range(2):
-                nc.vector.tensor_tensor(
-                    out=sq[g][:, c, j, :], in0=m_banks[g][j][:, c, :], in1=held[:, c, :], op=ALU.mult
-                )
+            c0 = vector_share(g, j)
+            twice = m_banks[g, j][:, :, :c0].unsqueeze(3).to_broadcast([P, 2, c0, 2])
+            nc.vector.tensor_reduce(out=sq[g][:, :, j, :c0], in_=twice, axis=mybir.AxisListType.X, op=ALU.mult)
+
+        def squares(g, part, cols):
+            return sq[g][:, part, :, :].rearrange("p j n -> p (j n)")[:, cols]
+
+        def add_on(engine, g, cols):
+            engine.tensor_tensor(out=power[g][:, cols], in0=squares(g, 0, cols), in1=squares(g, 1, cols), op=ALU.add)
 
         def add(g):
-            n = SIZES[g]
-            power[g] = pow_pool.tile([P, TILES, N], F32, name="power")
-            engine = nc.gpsimd if g < GROUPS - VECTOR_ADD_GROUPS else nc.vector
-            engine.tensor_tensor(
-                out=power[g][:, :n, :].rearrange("p j n -> p (j n)"),
-                in0=sq[g][:, 0, :n, :].rearrange("p j n -> p (j n)"),
-                in1=sq[g][:, 1, :n, :].rearrange("p j n -> p (j n)"),
-                op=ALU.add,
-            )
+            width = SIZES[g] * N
+            if g < VECTOR_ADD_GROUPS:
+                power[g] = squares(g, 0, slice(0, width))
+                add_on(nc.vector, g, slice(0, width))
+                return
+            v_cols = LAST_ADD_COLS if g == GROUPS - 2 else VECTOR_ADD_COLS if SIZES[g] == TILES else 0
+            power[g] = kt[g + 1][:, v_cols : v_cols + width]
+            if v_cols:
+                add_on(nc.vector, g, slice(width - v_cols, width))
+            add_on(nc.gpsimd, g, slice(0, width - v_cols))
 
-        def log_and_store(g):
-            n = SIZES[g]
-            res = out_pool.tile([P, TILES, N], F32, name="res")
-            nc.scalar.activation(out=res[:, :n, :], in_=power[g][:, :n, :], func=ACT.Ln)
-            rows = out[first_row[g] : first_row[g + 1], :]
-            nc.sync.dma_start(out=rows.rearrange("(p j) n -> p j n", j=n), in_=res[:, :n, :])
+        def log_and_store(g, tiles):
+            cols = slice(tiles.start * N, tiles.stop * N)
+            res = out_pool.tile([P, TILES * N], F32, name="res")
+            nc.scalar.activation(out=res[:, cols], in_=power[g][:, cols], func=ACT.Ln)
+            rows = out[first_row[g] : first_row[g + 1], :].rearrange("(p j) n -> p (j n)", j=SIZES[g])
+            nc.sync.dma_start(out=rows[:, cols], in_=res[:, cols])
 
         nc.sync.dma_start(out=w_raw[:, 0:2, :], in_=dft_real.rearrange("(j p) k -> p j k", p=P))
         nc.sync.dma_start(out=w_raw[:, 2:4, :], in_=dft_imag.rearrange("(j p) k -> p j k", p=P))
         for g in range(LOAD_AHEAD):
             load(g)
 
-        transpose("w", w_raw, TILES)
+        kt["w"] = new_kt()
+        transpose("w", w_raw, range(2))
         interleave("w", 0, True)
         interleave("w", 1, False)
-        transpose(0, raw[0], SIZES[0])
-        for half in range(SIZES[0] // 2):
-            interleave(0, half, True)
+        kt[0] = new_kt()
+        transpose(0, raw[0], range(SIZES[0] // 2))
+        for pair in range(SIZES[0] // 2):
+            interleave(0, pair, True)
         quantize_weights(0)
         quantize_weights(1)
 
-        for s in range(GROUPS + 2):
+        for s in range(GROUPS):
+            n = SIZES[s]
+            pairs = SIZES[s + 1] // 2 if s + 1 < GROUPS else 0
+            early, late = range(min(pairs, 2)), range(2, pairs)
+            v_tiles = [j for j in range(n) if vector_share(s, j)]
+            on_scalar = s + 1 < HEAD_COPY_GROUPS
             if s + LOAD_AHEAD < GROUPS:
                 load(s + LOAD_AHEAD)
-            if s + 1 < GROUPS:
-                transpose(s + 1, raw[s + 1], SIZES[s + 1])
-            if s < GROUPS:
+            if pairs:
+                kt[s + 1] = new_kt()
+                transpose(s + 1, raw[s + 1], early)
+            if n:
                 quantize(s)
             if 0 <= s - 1 < GROUPS:
                 add(s - 1)
-            if s < GROUPS:
-                multiply(s)
-            if s + 1 < GROUPS:
-                for half in range(SIZES[s + 1] // 2):
-                    interleave(s + 1, half, False)
-            if s < GROUPS:
-                for j in vector_tiles(s):
-                    square_on_vector(s, j)
+            if n:
+                sq[s] = sq_pool.tile([P, 2, TILES, N], F32, name="sq")
+                multiply(s, range(min(n, FIRST_RUN)))
+            for pair in early:
+                interleave(s + 1, pair, on_scalar)
+            if pairs:
+                transpose(s + 1, raw[s + 1], late)
             if 0 <= s - 2 < GROUPS:
-                log_and_store(s - 2)
-            if s < GROUPS:
-                for j in range(SIZES[s]):
-                    if j not in vector_tiles(s):
-                        square_on_scalar(s, j)
+                log_and_store(s - 2, range(SIZES[s - 2]))
+            for j in range(min(n, FIRST_RUN)):
+                square_on_scalar(s, j)
+            for j in v_tiles[:1]:
+                square_on_vector(s, j)
+            multiply(s, range(FIRST_RUN, n))
+            for j in range(FIRST_RUN, n):
+                square_on_scalar(s, j)
+            for pair in late:
+                interleave(s + 1, pair, on_scalar)
+            for j in v_tiles[1:]:
+                square_on_vector(s, j)
+
+        last = GROUPS - 1
+        for j0 in range(0, TILES, RUN):
+            log_and_store(last - 1, range(j0, j0 + RUN))
+        power[last] = squares(last, 0, slice(0, TILES * N))
+        for tiles in (range(0, 4), range(4, 6), range(6, 8)):
+            add_on(nc.vector, last, slice(tiles.start * N, tiles.stop * N))
+            log_and_store(last, tiles)

@@ -16,99 +16,98 @@ ACT = mybir.ActivationFunctionType
 ALU = mybir.AluOpType
 
 P = 128
-TILES = 8
-RUN = 4
+PAIR = 2
 WORDS = K // 2
-SIZES = [2, 2, 4] + [8] * 15
+SIZES = [1, 1] + [2] * 31
 GROUPS = len(SIZES)
-LOAD_AHEAD = 3
-HEAD_GROUPS = 3
-HEAD_COPY_GROUPS = 0
-VECTOR_ADD_GROUPS = 0
+PAIRS = sum(SIZES)
+MAX_PAIRS = 2
+TILES = MAX_PAIRS * PAIR
+LOAD_AHEAD = 4
+T_AHEAD = 1
+M_BEHIND = 2
+SQ_BEHIND = 3
+ADD_BEHIND = 2
+HEAD_PAIRS = 7
+TAIL_FROM = 62
 VECTOR_ADD_COLS = 256
-HALF_HEAD_GROUPS = 5
-LAST_VECTOR_TILES = (1, 3, 5)
-LAST_ADD_COLS = 768
-LAST_PIECES = 2
-SHARED_COLS = 192
+VECTOR_ADD_GROUPS = 1
+SHARED_COLS = 208
 T_BANKS = 2
 M_BANKS = 6
-FIRST_RUN = 5
-assert sum(SIZES) * P == B
+assert PAIRS * PAIR * P == B
 
 
 def tile_dft_kernel(tc, x, dft_real, dft_imag, out):
     nc = tc.nc
-    first_row = [sum(SIZES[:g]) * P for g in range(GROUPS + 1)]
+    first_pair = [sum(SIZES[:g]) for g in range(GROUPS + 1)]
+    group_of = [g for g in range(GROUPS) for i in range(SIZES[g])]
 
-    def vector_share(g, j):
-        if g < HEAD_GROUPS:
+    def vector_share(q):
+        if q < HEAD_PAIRS:
             return 0
-        if g == GROUPS - 1:
-            return N if j in LAST_VECTOR_TILES else 0
-        if j == 1:
-            return N
-        if g < HALF_HEAD_GROUPS:
-            return 0
-        if j == 4 and SIZES[g] == TILES:
-            return SHARED_COLS
-        return 0
+        if q >= TAIL_FROM:
+            return N if q in (PAIRS - 2,) else 0
+        return SHARED_COLS if q % 2 == (1) else 0
 
     with ExitStack() as ctx:
         keep = ctx.enter_context(tc.tile_pool(name="keep", bufs=1))
         raw_pool = ctx.enter_context(tc.tile_pool(name="raw", bufs=LOAD_AHEAD + 2))
         kt_pool = ctx.enter_context(tc.tile_pool(name="kt", bufs=4))
-        code_pool = ctx.enter_context(tc.tile_pool(name="code", bufs=2))
-        sq_pool = ctx.enter_context(tc.tile_pool(name="sq", bufs=3))
+        code_pool = ctx.enter_context(tc.tile_pool(name="code", bufs=3))
+        sq_pool = ctx.enter_context(tc.tile_pool(name="sq", bufs=4))
         tmp_pool = ctx.enter_context(tc.tile_pool(name="tmp", bufs=2))
-        out_pool = ctx.enter_context(tc.tile_pool(name="res", bufs=4))
+        out_pool = ctx.enter_context(tc.tile_pool(name="res", bufs=7))
         t_psum = ctx.enter_context(tc.psum_pool(name="t_psum", bufs=T_BANKS))
         m_psum = ctx.enter_context(tc.psum_pool(name="m_psum", bufs=M_BANKS))
         ctx.enter_context(tc.manual_schedule())
 
         ident = keep.tile([P, P], F32, name="ident")
         make_identity(nc, ident[:])
-        w_raw = keep.tile([P, RUN, K], BF16, name="w_raw")
+        w_raw = keep.tile([P, 2 * PAIR, K], BF16, name="w_raw")
+        w_kt = keep.tile([P, 2 * K], F32, name="w_kt", align_bytes=64)
         w_codes = keep.tile([P, 2 * N], U32, name="w_codes", align_bytes=64)
         w_scales = keep.tile([P, 2 * N], U8, name="w_scales", align_bytes=64)
 
         raw, t_banks, kt, codes, scales, m_banks, sq, power, held = {}, {}, {}, {}, {}, {}, {}, {}, {}
 
-        def new_kt():
-            return kt_pool.tile([P, TILES * WORDS + LAST_ADD_COLS], F32, name="kt", align_bytes=64)
-
         def load(g):
-            n = SIZES[g]
+            n = SIZES[g] * PAIR
             raw[g] = raw_pool.tile([P, TILES, K], BF16, name="x_raw")
-            rows = x[first_row[g] : first_row[g + 1], :]
+            rows = x[first_pair[g] * PAIR * P : first_pair[g + 1] * PAIR * P, :]
             nc.sync.dma_start(out=raw[g][:, :n, :], in_=rows.rearrange("(p j) k -> p j k", j=n))
 
-        def transpose(g, src, pairs):
+        def transpose(src, i):
             words = src[:].rearrange("p j k -> p (j k)").bitcast(F32)
-            for pair in pairs:
-                bank = t_psum.tile([P, 2, 2, P], F32, name="t_bank")
-                for jj in range(2):
-                    w0 = (2 * pair + jj) * WORDS
-                    for u in range(2):
-                        nc.tensor.transpose(bank[:, jj, u, :], words[:, w0 + u : w0 + WORDS : 2], ident[:])
-                t_banks[g, pair] = bank
+            bank = t_psum.tile([P, PAIR, 2, P], F32, name="t_bank")
+            for jj in range(PAIR):
+                w0 = (PAIR * i + jj) * WORDS
+                for u in range(2):
+                    nc.tensor.transpose(bank[:, jj, u, :], words[:, w0 + u : w0 + WORDS : 2], ident[:])
+            return bank
 
-        def interleave(g, pair, on_scalar):
-            dst = kt[g][:, pair * K : (pair + 1) * K].rearrange("p (j r u) -> p j r u", j=2, u=2)
-            src = t_banks[g, pair][:].rearrange("p j u r -> p j r u")
-            if on_scalar:
-                nc.scalar.copy(out=dst, in_=src)
-            else:
-                nc.vector.tensor_copy(out=dst, in_=src)
+        def transpose_x(q):
+            g = group_of[q]
+            t_banks[q] = transpose(raw[g], q - first_pair[g])
+
+        def interleave(copy, dst_tile, i, bank):
+            dst = dst_tile[:, i * K : (i + 1) * K].rearrange("p (j r u) -> p j r u", j=PAIR, u=2)
+            copy(out=dst, in_=bank[:].rearrange("p j u r -> p j r u"))
+
+        def interleave_x(copy, q):
+            g = group_of[q]
+            if q == first_pair[g]:
+                kt[g] = kt_pool.tile([P, TILES * WORDS + VECTOR_ADD_COLS], F32, name="kt", align_bytes=64)
+            interleave(copy, kt[g][:, VECTOR_ADD_COLS:], q - first_pair[g], t_banks[q])
 
         def quantize(g):
-            n = SIZES[g]
+            n = SIZES[g] * PAIR
             codes[g] = code_pool.tile([P, TILES * P], U32, name="x_codes", align_bytes=64)
             scales[g] = code_pool.tile([P, TILES * P], U8, name="x_scales", align_bytes=64)
             nc.vector.quantize_mx(
                 out=codes[g][:, : n * P].bitcast(E5M2X4),
                 scales=scales[g][:, : n * P],
-                in_=kt[g][:, : n * WORDS].bitcast(BF16),
+                in_=kt[g][:, VECTOR_ADD_COLS : VECTOR_ADD_COLS + n * WORDS].bitcast(BF16),
             )
 
         def quantize_weights(half):
@@ -116,11 +115,13 @@ def tile_dft_kernel(tc, x, dft_real, dft_imag, out):
             nc.vector.quantize_mx(
                 out=w_codes[:, cols].bitcast(E4M3X4),
                 scales=w_scales[:, cols],
-                in_=kt["w"][:, half * K : (half + 1) * K].bitcast(BF16),
+                in_=w_kt[:, half * K : (half + 1) * K].bitcast(BF16),
             )
 
-        def multiply(g, tiles):
-            for j in tiles:
+        def multiply(q):
+            g = group_of[q]
+            for jj in range(PAIR):
+                j = (q - first_pair[g]) * PAIR + jj
                 bank = m_psum.tile([P, 2, N], F32, name="m_bank")
                 cols = slice(j * P, (j + 1) * P)
                 nc.tensor.matmul_mx(
@@ -132,17 +133,36 @@ def tile_dft_kernel(tc, x, dft_real, dft_imag, out):
                     start=True,
                     stop=True,
                 )
-                m_banks[g, j] = bank
+                m_banks[q, jj] = bank
 
-        def square_on_scalar(g, j):
-            c0 = vector_share(g, j)
-            if c0 < N:
-                nc.scalar.activation(out=sq[g][:, :, j, c0:], in_=m_banks[g, j][:, :, c0:], func=ACT.Square)
+        def square_on_scalar(q, jj):
+            g = group_of[q]
+            if g not in sq:
+                sq[g] = sq_pool.tile([P, 2, TILES, N], F32, name="sq")
+            j = (q - first_pair[g]) * PAIR + jj
+            c0 = vector_share(q) if jj == 0 else 0
+            if c0 < N and (q, jj) not in done:
+                nc.scalar.activation(out=sq[g][:, :, j, c0:], in_=m_banks[q, jj][:, :, c0:], func=ACT.Square)
+                done.add((q, jj))
 
-        def square_on_vector(g, j):
-            c0 = vector_share(g, j)
-            twice = m_banks[g, j][:, :, :c0].unsqueeze(3).to_broadcast([P, 2, c0, 2])
-            nc.vector.tensor_reduce(out=sq[g][:, :, j, :c0], in_=twice, axis=mybir.AxisListType.X, op=ALU.mult)
+        def squares_on_scalar(q):
+            for jj in range(PAIR):
+                square_on_scalar(q, jj)
+            if (q + 1, 0) in m_banks and vector_share(q + 1):
+                square_on_scalar(q + 1, 0)
+
+        def hold(q):
+            c0 = vector_share(q)
+            held[q] = tmp_pool.tile([P, 2, N], F32, name="held")
+            nc.vector.tensor_copy(out=held[q][:, :, :c0], in_=m_banks[q, 0][:, :, :c0])
+
+        def square_on_vector(q):
+            g = group_of[q]
+            c0 = vector_share(q)
+            j = (q - first_pair[g]) * PAIR
+            nc.vector.tensor_tensor(
+                out=sq[g][:, :, j, :c0], in0=m_banks[q, 0][:, :, :c0], in1=held[q][:, :, :c0], op=ALU.mult
+            )
 
         def squares(g, part, cols):
             return sq[g][:, part, :, :].rearrange("p j n -> p (j n)")[:, cols]
@@ -150,81 +170,81 @@ def tile_dft_kernel(tc, x, dft_real, dft_imag, out):
         def add_on(engine, g, cols):
             engine.tensor_tensor(out=power[g][:, cols], in0=squares(g, 0, cols), in1=squares(g, 1, cols), op=ALU.add)
 
-        def add(g):
-            width = SIZES[g] * N
-            if g < VECTOR_ADD_GROUPS:
-                power[g] = squares(g, 0, slice(0, width))
-                add_on(nc.vector, g, slice(0, width))
-                return
-            v_cols = LAST_ADD_COLS if g == GROUPS - 2 else VECTOR_ADD_COLS if SIZES[g] == TILES else 0
-            power[g] = kt[g + 1][:, v_cols : v_cols + width]
+        def add(g, host):
+            width = SIZES[g] * PAIR * N
+            v_cols = VECTOR_ADD_COLS if SIZES[g] == MAX_PAIRS else 0
+            power[g] = host[:, VECTOR_ADD_COLS - v_cols : VECTOR_ADD_COLS - v_cols + width]
             if v_cols:
-                add_on(nc.vector, g, slice(width - v_cols, width))
-            add_on(nc.gpsimd, g, slice(0, width - v_cols))
+                add_on(nc.vector, g, slice(0, v_cols))
+            add_on(nc.gpsimd, g, slice(v_cols, width))
 
         def log_and_store(g, tiles):
             cols = slice(tiles.start * N, tiles.stop * N)
             res = out_pool.tile([P, TILES * N], F32, name="res")
             nc.scalar.activation(out=res[:, cols], in_=power[g][:, cols], func=ACT.Ln)
-            rows = out[first_row[g] : first_row[g + 1], :].rearrange("(p j) n -> p (j n)", j=SIZES[g])
-            nc.sync.dma_start(out=rows[:, cols], in_=res[:, cols])
+            rows = out[first_pair[g] * PAIR * P : first_pair[g + 1] * PAIR * P, :]
+            nc.sync.dma_start(out=rows.rearrange("(p j) n -> p (j n)", j=SIZES[g] * PAIR)[:, cols], in_=res[:, cols])
 
         nc.sync.dma_start(out=w_raw[:, 0:2, :], in_=dft_real.rearrange("(j p) k -> p j k", p=P))
         nc.sync.dma_start(out=w_raw[:, 2:4, :], in_=dft_imag.rearrange("(j p) k -> p j k", p=P))
         for g in range(LOAD_AHEAD):
             load(g)
 
-        kt["w"] = new_kt()
-        transpose("w", w_raw, range(2))
-        interleave("w", 0, True)
-        interleave("w", 1, False)
-        kt[0] = new_kt()
-        transpose(0, raw[0], range(SIZES[0] // 2))
-        for pair in range(SIZES[0] // 2):
-            interleave(0, pair, True)
+        interleave(nc.scalar.copy, w_kt, 0, transpose(w_raw, 0))
+        interleave(nc.vector.tensor_copy, w_kt, 1, transpose(w_raw, 1))
+        for q in range(SIZES[0]):
+            transpose_x(q)
+            interleave_x(nc.scalar.copy, q)
         quantize_weights(0)
         quantize_weights(1)
+        for q in range(SIZES[0], SIZES[0] + T_AHEAD):
+            transpose_x(q)
 
+        done = set()
+        m_next, sq_next, add_next, log_next = 0, 0, 0, 0
+        pending = []
         for s in range(GROUPS):
-            n = SIZES[s]
-            pairs = SIZES[s + 1] // 2 if s + 1 < GROUPS else 0
-            early, late = range(min(pairs, 2)), range(2, pairs)
-            v_tiles = [j for j in range(n) if vector_share(s, j)]
-            on_scalar = s + 1 < HEAD_COPY_GROUPS
             if s + LOAD_AHEAD < GROUPS:
                 load(s + LOAD_AHEAD)
-            if pairs:
-                kt[s + 1] = new_kt()
-                transpose(s + 1, raw[s + 1], early)
-            if n:
-                quantize(s)
-            if 0 <= s - 1 < GROUPS:
-                add(s - 1)
-            if n:
-                sq[s] = sq_pool.tile([P, 2, TILES, N], F32, name="sq")
-                multiply(s, range(min(n, FIRST_RUN)))
-            for pair in early:
-                interleave(s + 1, pair, on_scalar)
-            if pairs:
-                transpose(s + 1, raw[s + 1], late)
-            if 0 <= s - 2 < GROUPS:
-                log_and_store(s - 2, range(SIZES[s - 2]))
-            for j in range(min(n, FIRST_RUN)):
-                square_on_scalar(s, j)
-            for j in v_tiles[:1]:
-                square_on_vector(s, j)
-            multiply(s, range(FIRST_RUN, n))
-            for j in range(FIRST_RUN, n):
-                square_on_scalar(s, j)
-            for pair in late:
-                interleave(s + 1, pair, on_scalar)
-            for j in v_tiles[1:]:
-                square_on_vector(s, j)
+            quantize(s)
+            ready = add_next < GROUPS and sq_next >= first_pair[add_next + 1] and not [r for r in pending if group_of[r] == add_next]
+            logs = range(log_next, add_next)
+            if ready:
+                add(add_next, kt[s])
+                add_next += 1
+            for g in logs:
+                log_and_store(g, range(SIZES[g] * PAIR))
+                log_next += 1
+            slots = range(first_pair[s + 1], first_pair[s + 2]) if s + 1 < GROUPS else range(PAIRS, PAIRS + MAX_PAIRS)
+            for q in slots:
+                if q + T_AHEAD < PAIRS and s >= 2:
+                    transpose_x(q + T_AHEAD)
+                m_last = first_pair[s + 1] - 1 if q == slots[-1] else min(first_pair[s] + q - slots[0], first_pair[s + 1] - 1)
+                while m_next <= m_last:
+                    multiply(m_next)
+                    m_next += 1
+                if q + T_AHEAD < PAIRS and s < 2:
+                    transpose_x(q + T_AHEAD)
+                if q < PAIRS:
+                    interleave_x(nc.vector.tensor_copy, q)
+                for r in pending:
+                    square_on_vector(r)
+                pending = []
+                while sq_next < m_next - (0 if sq_next < 2 else 1):
+                    squares_on_scalar(sq_next)
+                    if vector_share(sq_next):
+                        hold(sq_next)
+                        pending.append(sq_next)
+                    sq_next += 1
 
-        last = GROUPS - 1
-        for j0 in range(0, TILES, RUN):
-            log_and_store(last - 1, range(j0, j0 + RUN))
-        power[last] = squares(last, 0, slice(0, TILES * N))
-        for tiles in (range(0, 4), range(4, 6), range(6, 8)):
-            add_on(nc.vector, last, slice(tiles.start * N, tiles.stop * N))
-            log_and_store(last, tiles)
+        for r in pending:
+            square_on_vector(r)
+        for g in range(log_next, add_next):
+            log_and_store(g, range(SIZES[g] * PAIR))
+        for q in range(sq_next, PAIRS):
+            squares_on_scalar(q)
+        for g in range(add_next, GROUPS):
+            power[g] = squares(g, 0, slice(0, SIZES[g] * PAIR * N))
+            for tiles in (range(0, 2), range(2, 4)) if g < GROUPS - 1 else (range(0, 2), range(2, 4)):
+                add_on(nc.vector, g, slice(tiles.start * N, tiles.stop * N))
+                log_and_store(g, tiles)

@@ -18,23 +18,18 @@ ALU = mybir.AluOpType
 P = 128
 PAIR = 2
 WORDS = K // 2
-SIZES = [1, 1] + [2] * 31
+TILES = 2 * PAIR
+SHORT_GROUPS = 2
+SIZES = [1] * SHORT_GROUPS + [2] * 31
 GROUPS = len(SIZES)
 PAIRS = sum(SIZES)
-MAX_PAIRS = 2
-TILES = MAX_PAIRS * PAIR
 LOAD_AHEAD = 4
-T_AHEAD = 1
-M_BEHIND = 2
-SQ_BEHIND = 3
-ADD_BEHIND = 2
-HEAD_PAIRS = 7
-TAIL_FROM = 62
-VECTOR_ADD_COLS = 256
-VECTOR_ADD_GROUPS = 1
-SHARED_COLS = 208
-T_BANKS = 2
-M_BANKS = 6
+
+VECTOR_SQUARE_COLS = 240
+VECTOR_ADD_COLS = 128
+SCALAR_ONLY_PAIRS = 7
+TAIL_PAIRS = 3
+T_BANKS, M_BANKS = 2, 6
 assert PAIRS * PAIR * P == B
 
 
@@ -43,12 +38,13 @@ def tile_dft_kernel(tc, x, dft_real, dft_imag, out):
     first_pair = [sum(SIZES[:g]) for g in range(GROUPS + 1)]
     group_of = [g for g in range(GROUPS) for i in range(SIZES[g])]
 
-    def vector_share(q):
-        if q < HEAD_PAIRS:
-            return 0
-        if q >= TAIL_FROM:
-            return N if q in (PAIRS - 2,) else 0
-        return SHARED_COLS if q % 2 == (1) else 0
+    def vector_cols(q):
+        if q >= PAIRS - TAIL_PAIRS:
+            return N
+        return VECTOR_SQUARE_COLS if q >= SCALAR_ONLY_PAIRS and q % 2 == 1 else 0
+
+    def sum_step(g):
+        return g + 1 if g < SHORT_GROUPS else g + 2
 
     with ExitStack() as ctx:
         keep = ctx.enter_context(tc.tile_pool(name="keep", bufs=1))
@@ -56,26 +52,28 @@ def tile_dft_kernel(tc, x, dft_real, dft_imag, out):
         kt_pool = ctx.enter_context(tc.tile_pool(name="kt", bufs=4))
         code_pool = ctx.enter_context(tc.tile_pool(name="code", bufs=3))
         sq_pool = ctx.enter_context(tc.tile_pool(name="sq", bufs=4))
-        tmp_pool = ctx.enter_context(tc.tile_pool(name="tmp", bufs=2))
-        out_pool = ctx.enter_context(tc.tile_pool(name="res", bufs=7))
+        held_pool = ctx.enter_context(tc.tile_pool(name="held", bufs=2))
+        res_pool = ctx.enter_context(tc.tile_pool(name="res", bufs=7))
         t_psum = ctx.enter_context(tc.psum_pool(name="t_psum", bufs=T_BANKS))
         m_psum = ctx.enter_context(tc.psum_pool(name="m_psum", bufs=M_BANKS))
         ctx.enter_context(tc.manual_schedule())
 
         ident = keep.tile([P, P], F32, name="ident")
         make_identity(nc, ident[:])
-        w_raw = keep.tile([P, 2 * PAIR, K], BF16, name="w_raw")
-        w_kt = keep.tile([P, 2 * K], F32, name="w_kt", align_bytes=64)
+        w_raw = keep.tile([P, TILES, K], BF16, name="w_raw")
+        w_kt = keep.tile([P, TILES * WORDS], F32, name="w_kt", align_bytes=64)
         w_codes = keep.tile([P, 2 * N], U32, name="w_codes", align_bytes=64)
         w_scales = keep.tile([P, 2 * N], U8, name="w_scales", align_bytes=64)
 
-        raw, t_banks, kt, codes, scales, m_banks, sq, power, held = {}, {}, {}, {}, {}, {}, {}, {}, {}
+        raw, t_banks, kt, codes, scales, m_banks, sq, held, power = {}, {}, {}, {}, {}, {}, {}, {}, {}
+
+        def group_rows(g):
+            return slice(first_pair[g] * PAIR * P, first_pair[g + 1] * PAIR * P)
 
         def load(g):
             n = SIZES[g] * PAIR
             raw[g] = raw_pool.tile([P, TILES, K], BF16, name="x_raw")
-            rows = x[first_pair[g] * PAIR * P : first_pair[g + 1] * PAIR * P, :]
-            nc.sync.dma_start(out=raw[g][:, :n, :], in_=rows.rearrange("(p j) k -> p j k", j=n))
+            nc.sync.dma_start(out=raw[g][:, :n, :], in_=x[group_rows(g), :].rearrange("(p j) k -> p j k", j=n))
 
         def transpose(src, i):
             words = src[:].rearrange("p j k -> p (j k)").bitcast(F32)
@@ -86,19 +84,29 @@ def tile_dft_kernel(tc, x, dft_real, dft_imag, out):
                     nc.tensor.transpose(bank[:, jj, u, :], words[:, w0 + u : w0 + WORDS : 2], ident[:])
             return bank
 
+        def interleave(copy, words, i, bank):
+            width = PAIR * WORDS
+            dst = words[:, i * width : (i + 1) * width].rearrange("p (j r u) -> p j r u", j=PAIR, u=2)
+            copy(out=dst, in_=bank[:].rearrange("p j u r -> p j r u"))
+
         def transpose_x(q):
             g = group_of[q]
             t_banks[q] = transpose(raw[g], q - first_pair[g])
 
-        def interleave(copy, dst_tile, i, bank):
-            dst = dst_tile[:, i * K : (i + 1) * K].rearrange("p (j r u) -> p j r u", j=PAIR, u=2)
-            copy(out=dst, in_=bank[:].rearrange("p j u r -> p j r u"))
-
         def interleave_x(copy, q):
             g = group_of[q]
             if q == first_pair[g]:
-                kt[g] = kt_pool.tile([P, TILES * WORDS + VECTOR_ADD_COLS], F32, name="kt", align_bytes=64)
+                kt[g] = kt_pool.tile([P, VECTOR_ADD_COLS + TILES * WORDS], F32, name="kt", align_bytes=64)
             interleave(copy, kt[g][:, VECTOR_ADD_COLS:], q - first_pair[g], t_banks[q])
+
+        def quantize_weights(half):
+            cols = slice(half * N, (half + 1) * N)
+            width = PAIR * WORDS
+            nc.vector.quantize_mx(
+                out=w_codes[:, cols].bitcast(E4M3X4),
+                scales=w_scales[:, cols],
+                in_=w_kt[:, half * width : (half + 1) * width].bitcast(BF16),
+            )
 
         def quantize(g):
             n = SIZES[g] * PAIR
@@ -110,20 +118,15 @@ def tile_dft_kernel(tc, x, dft_real, dft_imag, out):
                 in_=kt[g][:, VECTOR_ADD_COLS : VECTOR_ADD_COLS + n * WORDS].bitcast(BF16),
             )
 
-        def quantize_weights(half):
-            cols = slice(half * N, (half + 1) * N)
-            nc.vector.quantize_mx(
-                out=w_codes[:, cols].bitcast(E4M3X4),
-                scales=w_scales[:, cols],
-                in_=w_kt[:, half * K : (half + 1) * K].bitcast(BF16),
-            )
+        def tile_in_group(q, jj):
+            return (q - first_pair[group_of[q]]) * PAIR + jj
 
         def multiply(q):
             g = group_of[q]
             for jj in range(PAIR):
-                j = (q - first_pair[g]) * PAIR + jj
-                bank = m_psum.tile([P, 2, N], F32, name="m_bank")
+                j = tile_in_group(q, jj)
                 cols = slice(j * P, (j + 1) * P)
+                bank = m_psum.tile([P, 2, N], F32, name="m_bank")
                 nc.tensor.matmul_mx(
                     out=bank[:].rearrange("p c n -> p (c n)"),
                     lhsT=codes[g][:, cols].bitcast(E5M2X4),
@@ -135,116 +138,117 @@ def tile_dft_kernel(tc, x, dft_real, dft_imag, out):
                 )
                 m_banks[q, jj] = bank
 
-        def square_on_scalar(q, jj):
-            g = group_of[q]
-            if g not in sq:
-                sq[g] = sq_pool.tile([P, 2, TILES, N], F32, name="sq")
-            j = (q - first_pair[g]) * PAIR + jj
-            c0 = vector_share(q) if jj == 0 else 0
-            if c0 < N and (q, jj) not in done:
-                nc.scalar.activation(out=sq[g][:, :, j, c0:], in_=m_banks[q, jj][:, :, c0:], func=ACT.Square)
-                done.add((q, jj))
+        def square_bank(q, jj, c0):
+            j = tile_in_group(q, jj)
+            nc.scalar.activation(out=sq[group_of[q]][:, :, j, c0:], in_=m_banks[q, jj][:, :, c0:], func=ACT.Square)
 
-        def squares_on_scalar(q):
+        def square_on_scalar(q):
+            g = group_of[q]
+            if q == first_pair[g]:
+                sq[g] = sq_pool.tile([P, 2, TILES, N], F32, name="sq")
             for jj in range(PAIR):
-                square_on_scalar(q, jj)
-            if (q + 1, 0) in m_banks and vector_share(q + 1):
-                square_on_scalar(q + 1, 0)
+                if jj > 0 or not vector_cols(q):
+                    square_bank(q, jj, 0)
+            if q + 1 < PAIRS and 0 < vector_cols(q + 1) < N:
+                square_bank(q + 1, 0, vector_cols(q + 1))
 
         def hold(q):
-            c0 = vector_share(q)
-            held[q] = tmp_pool.tile([P, 2, N], F32, name="held")
+            c0 = vector_cols(q)
+            held[q] = held_pool.tile([P, 2, N], F32, name="held")
             nc.vector.tensor_copy(out=held[q][:, :, :c0], in_=m_banks[q, 0][:, :, :c0])
 
         def square_on_vector(q):
-            g = group_of[q]
-            c0 = vector_share(q)
-            j = (q - first_pair[g]) * PAIR
+            c0 = vector_cols(q)
             nc.vector.tensor_tensor(
-                out=sq[g][:, :, j, :c0], in0=m_banks[q, 0][:, :, :c0], in1=held[q][:, :, :c0], op=ALU.mult
+                out=sq[group_of[q]][:, :, tile_in_group(q, 0), :c0],
+                in0=m_banks[q, 0][:, :, :c0],
+                in1=held[q][:, :, :c0],
+                op=ALU.mult,
             )
 
-        def squares(g, part, cols):
-            return sq[g][:, part, :, :].rearrange("p j n -> p (j n)")[:, cols]
+        def squares(g, part):
+            return sq[g][:, part, :, :].rearrange("p j n -> p (j n)")
 
         def add_on(engine, g, cols):
-            engine.tensor_tensor(out=power[g][:, cols], in0=squares(g, 0, cols), in1=squares(g, 1, cols), op=ALU.add)
+            engine.tensor_tensor(
+                out=power[g][:, cols], in0=squares(g, 0)[:, cols], in1=squares(g, 1)[:, cols], op=ALU.add
+            )
 
-        def add(g, host):
+        def add(g, s):
             width = SIZES[g] * PAIR * N
-            v_cols = VECTOR_ADD_COLS if SIZES[g] == MAX_PAIRS else 0
-            power[g] = host[:, VECTOR_ADD_COLS - v_cols : VECTOR_ADD_COLS - v_cols + width]
+            v_cols = VECTOR_ADD_COLS if g >= SHORT_GROUPS else 0
+            start = VECTOR_ADD_COLS - v_cols
+            power[g] = kt[s][:, start : start + width]
             if v_cols:
                 add_on(nc.vector, g, slice(0, v_cols))
             add_on(nc.gpsimd, g, slice(v_cols, width))
 
         def log_and_store(g, tiles):
             cols = slice(tiles.start * N, tiles.stop * N)
-            res = out_pool.tile([P, TILES * N], F32, name="res")
+            res = res_pool.tile([P, TILES * N], F32, name="res")
             nc.scalar.activation(out=res[:, cols], in_=power[g][:, cols], func=ACT.Ln)
-            rows = out[first_pair[g] * PAIR * P : first_pair[g + 1] * PAIR * P, :]
-            nc.sync.dma_start(out=rows.rearrange("(p j) n -> p (j n)", j=SIZES[g] * PAIR)[:, cols], in_=res[:, cols])
+            rows = out[group_rows(g), :].rearrange("(p j) n -> p (j n)", j=SIZES[g] * PAIR)
+            nc.sync.dma_start(out=rows[:, cols], in_=res[:, cols])
 
-        nc.sync.dma_start(out=w_raw[:, 0:2, :], in_=dft_real.rearrange("(j p) k -> p j k", p=P))
-        nc.sync.dma_start(out=w_raw[:, 2:4, :], in_=dft_imag.rearrange("(j p) k -> p j k", p=P))
+        nc.sync.dma_start(out=w_raw[:, :PAIR, :], in_=dft_real.rearrange("(j p) k -> p j k", p=P))
+        nc.sync.dma_start(out=w_raw[:, PAIR:, :], in_=dft_imag.rearrange("(j p) k -> p j k", p=P))
         for g in range(LOAD_AHEAD):
             load(g)
-
         interleave(nc.scalar.copy, w_kt, 0, transpose(w_raw, 0))
         interleave(nc.vector.tensor_copy, w_kt, 1, transpose(w_raw, 1))
-        for q in range(SIZES[0]):
-            transpose_x(q)
-            interleave_x(nc.scalar.copy, q)
+        transpose_x(0)
+        interleave_x(nc.scalar.copy, 0)
         quantize_weights(0)
         quantize_weights(1)
-        for q in range(SIZES[0], SIZES[0] + T_AHEAD):
-            transpose_x(q)
+        transpose_x(1)
 
-        done = set()
-        m_next, sq_next, add_next, log_next = 0, 0, 0, 0
-        pending = []
         for s in range(GROUPS):
             if s + LOAD_AHEAD < GROUPS:
                 load(s + LOAD_AHEAD)
             quantize(s)
-            ready = add_next < GROUPS and sq_next >= first_pair[add_next + 1] and not [r for r in pending if group_of[r] == add_next]
-            logs = range(log_next, add_next)
-            if ready:
-                add(add_next, kt[s])
-                add_next += 1
-            for g in logs:
-                log_and_store(g, range(SIZES[g] * PAIR))
-                log_next += 1
-            slots = range(first_pair[s + 1], first_pair[s + 2]) if s + 1 < GROUPS else range(PAIRS, PAIRS + MAX_PAIRS)
-            for q in slots:
-                if q + T_AHEAD < PAIRS and s >= 2:
-                    transpose_x(q + T_AHEAD)
-                m_last = first_pair[s + 1] - 1 if q == slots[-1] else min(first_pair[s] + q - slots[0], first_pair[s + 1] - 1)
-                while m_next <= m_last:
-                    multiply(m_next)
-                    m_next += 1
-                if q + T_AHEAD < PAIRS and s < 2:
-                    transpose_x(q + T_AHEAD)
-                if q < PAIRS:
-                    interleave_x(nc.vector.tensor_copy, q)
-                for r in pending:
-                    square_on_vector(r)
-                pending = []
-                while sq_next < m_next - (0 if sq_next < 2 else 1):
-                    squares_on_scalar(sq_next)
-                    if vector_share(sq_next):
-                        hold(sq_next)
-                        pending.append(sq_next)
-                    sq_next += 1
+            for g in range(s):
+                if sum_step(g) == s:
+                    add(g, s)
+            for g in range(s):
+                if sum_step(g) + 1 == s:
+                    log_and_store(g, range(SIZES[g] * PAIR))
+            for i in range(SIZES[s + 1] if s + 1 < GROUPS else 0):
+                q = first_pair[s + 1] + i
+                m = first_pair[s] + i if i < SIZES[s] else None
+                if s == 0:
+                    multiply(m)
+                if q + 1 < PAIRS:
+                    transpose_x(q + 1)
+                if s > 0 and m is not None:
+                    multiply(m)
+                interleave_x(nc.vector.tensor_copy, q)
+                if m is None:
+                    continue
+                if m - 2 in held:
+                    square_on_vector(m - 2)
+                if m < SHORT_GROUPS:
+                    square_on_scalar(m)
+                elif m > SHORT_GROUPS:
+                    square_on_scalar(m - 1)
+                    if vector_cols(m - 1):
+                        hold(m - 1)
 
-        for r in pending:
-            square_on_vector(r)
-        for g in range(log_next, add_next):
-            log_and_store(g, range(SIZES[g] * PAIR))
-        for q in range(sq_next, PAIRS):
-            squares_on_scalar(q)
-        for g in range(add_next, GROUPS):
-            power[g] = squares(g, 0, slice(0, SIZES[g] * PAIR * N))
-            for tiles in (range(0, 2), range(2, 4)) if g < GROUPS - 1 else (range(0, 2), range(2, 4)):
-                add_on(nc.vector, g, slice(tiles.start * N, tiles.stop * N))
-                log_and_store(g, tiles)
+        a, b, c = range(PAIRS - TAIL_PAIRS, PAIRS)
+        multiply(b)
+        hold(a)
+        square_on_scalar(a)
+        hold(b)
+        square_on_vector(a)
+        multiply(c)
+        square_on_scalar(b)
+        hold(c)
+        square_on_vector(b)
+        square_on_scalar(c)
+        square_on_vector(c)
+        log_and_store(GROUPS - 3, range(TILES))
+        for g in (GROUPS - 2, GROUPS - 1):
+            power[g] = squares(g, 0)
+            for j0 in range(0, TILES, PAIR):
+                engine = nc.gpsimd if (g, j0) == (GROUPS - 2, 0) else nc.vector
+                add_on(engine, g, slice(j0 * N, (j0 + PAIR) * N))
+                log_and_store(g, range(j0, j0 + PAIR))

@@ -25,11 +25,11 @@ GROUPS = len(SIZES)
 PAIRS = sum(SIZES)
 LOAD_AHEAD = 4
 
-VECTOR_SQUARE_COLS = 240
-VECTOR_ADD_COLS = 128
+VECTOR_SQUARE_COLS = 208
+VECTOR_ADD_COLS = 256
 SCALAR_ONLY_PAIRS = 7
-TAIL_PAIRS = 3
 T_BANKS, M_BANKS = 2, 6
+WARM_FIRST, WARM_SECOND = 5, 2
 assert PAIRS * PAIR * P == B
 
 
@@ -39,8 +39,8 @@ def tile_dft_kernel(tc, x, dft_real, dft_imag, out):
     group_of = [g for g in range(GROUPS) for i in range(SIZES[g])]
 
     def vector_cols(q):
-        if q >= PAIRS - TAIL_PAIRS:
-            return N
+        if q >= first_pair[GROUPS - 1]:
+            return N if q == first_pair[GROUPS - 1] else 0
         return VECTOR_SQUARE_COLS if q >= SCALAR_ONLY_PAIRS and q % 2 == 1 else 0
 
     def sum_step(g):
@@ -57,6 +57,20 @@ def tile_dft_kernel(tc, x, dft_real, dft_imag, out):
         t_psum = ctx.enter_context(tc.psum_pool(name="t_psum", bufs=T_BANKS))
         m_psum = ctx.enter_context(tc.psum_pool(name="m_psum", bufs=M_BANKS))
         ctx.enter_context(tc.manual_schedule())
+
+        warm = keep.tile([P, 2 * N], BF16, name="warm")
+        warm_log = keep.tile([P, 1], F32, name="warm_log")
+        nc.vector.memset(warm[:], 1.0)
+        nc.scalar.activation(out=warm_log[:], in_=warm[:, 0:1], func=ACT.Ln)
+
+        def warm_up(count):
+            bank = m_psum.tile([P, 2, N], F32, name="m_bank")
+            for i in range(count):
+                nc.tensor.matmul(
+                    out=bank[:].rearrange("p c n -> p (c n)"), lhsT=warm[:, :P], rhs=warm[:], start=True, stop=True
+                )
+
+        warm_up(WARM_FIRST)
 
         ident = keep.tile([P, P], F32, name="ident")
         make_identity(nc, ident[:])
@@ -196,6 +210,7 @@ def tile_dft_kernel(tc, x, dft_real, dft_imag, out):
             load(g)
         interleave(nc.scalar.copy, w_kt, 0, transpose(w_raw, 0))
         interleave(nc.vector.tensor_copy, w_kt, 1, transpose(w_raw, 1))
+        warm_up(WARM_SECOND)
         transpose_x(0)
         interleave_x(nc.scalar.copy, 0)
         quantize_weights(0)
@@ -215,11 +230,11 @@ def tile_dft_kernel(tc, x, dft_real, dft_imag, out):
             for i in range(SIZES[s + 1] if s + 1 < GROUPS else 0):
                 q = first_pair[s + 1] + i
                 m = first_pair[s] + i if i < SIZES[s] else None
-                if s == 0:
+                if s < SHORT_GROUPS and m is not None:
                     multiply(m)
                 if q + 1 < PAIRS:
                     transpose_x(q + 1)
-                if s > 0 and m is not None:
+                if s >= SHORT_GROUPS:
                     multiply(m)
                 interleave_x(nc.vector.tensor_copy, q)
                 if m is None:
@@ -233,22 +248,19 @@ def tile_dft_kernel(tc, x, dft_real, dft_imag, out):
                     if vector_cols(m - 1):
                         hold(m - 1)
 
-        a, b, c = range(PAIRS - TAIL_PAIRS, PAIRS)
-        multiply(b)
-        hold(a)
-        square_on_scalar(a)
-        hold(b)
-        square_on_vector(a)
-        multiply(c)
-        square_on_scalar(b)
-        hold(c)
-        square_on_vector(b)
-        square_on_scalar(c)
-        square_on_vector(c)
+        before, first, second = range(PAIRS - 3, PAIRS)
+        multiply(first)
+        square_on_scalar(before)
+        hold(before)
+        multiply(second)
+        square_on_vector(before)
+        square_on_scalar(first)
+        hold(first)
+        square_on_vector(first)
         log_and_store(GROUPS - 3, range(TILES))
+        square_on_scalar(second)
         for g in (GROUPS - 2, GROUPS - 1):
             power[g] = squares(g, 0)
             for j0 in range(0, TILES, PAIR):
-                engine = nc.gpsimd if (g, j0) == (GROUPS - 2, 0) else nc.vector
-                add_on(engine, g, slice(j0 * N, (j0 + PAIR) * N))
+                add_on(nc.vector, g, slice(j0 * N, (j0 + PAIR) * N))
                 log_and_store(g, range(j0, j0 + PAIR))

from contextlib import ExitStack

import concourse.mybir as mybir
from concourse.masks import make_identity

B, K, N = 16384, 512, 256
FLOPS = 2 * B * K * 2 * N

F32 = mybir.dt.float32
BF16 = mybir.dt.bfloat16
U32 = mybir.dt.uint32
U8 = mybir.dt.uint8
E4M3X4 = mybir.dt.float8_e4m3fn_x4
E5M2X4 = mybir.dt.float8_e5m2_x4
ACT = mybir.ActivationFunctionType
ALU = mybir.AluOpType

P = 128
PAIR = 2
WORDS = K // 2
TILES = 2 * PAIR
SHORT_GROUPS = 2
SIZES = [1] * SHORT_GROUPS + [2] * 31
GROUPS = len(SIZES)
PAIRS = sum(SIZES)
LOAD_AHEAD = 4

VECTOR_SQUARE_COLS = 208
VECTOR_ADD_COLS = 256
SCALAR_ONLY_PAIRS = 7
T_BANKS, M_BANKS = 2, 6
WARM_FIRST, WARM_SECOND = 5, 2
assert PAIRS * PAIR * P == B


def tile_dft_kernel(tc, x, dft_real, dft_imag, out):
    nc = tc.nc
    first_pair = [sum(SIZES[:g]) for g in range(GROUPS + 1)]
    group_of = [g for g in range(GROUPS) for i in range(SIZES[g])]

    def vector_cols(q):
        if q >= first_pair[GROUPS - 1]:
            return N if q == first_pair[GROUPS - 1] else 0
        return VECTOR_SQUARE_COLS if q >= SCALAR_ONLY_PAIRS and q % 2 == 1 else 0

    def sum_step(g):
        return g + 1 if g < SHORT_GROUPS else g + 2

    with ExitStack() as ctx:
        keep = ctx.enter_context(tc.tile_pool(name="keep", bufs=1))
        raw_pool = ctx.enter_context(tc.tile_pool(name="raw", bufs=LOAD_AHEAD + 2))
        kt_pool = ctx.enter_context(tc.tile_pool(name="kt", bufs=4))
        code_pool = ctx.enter_context(tc.tile_pool(name="code", bufs=3))
        sq_pool = ctx.enter_context(tc.tile_pool(name="sq", bufs=4))
        held_pool = ctx.enter_context(tc.tile_pool(name="held", bufs=2))
        res_pool = ctx.enter_context(tc.tile_pool(name="res", bufs=7))
        t_psum = ctx.enter_context(tc.psum_pool(name="t_psum", bufs=T_BANKS))
        m_psum = ctx.enter_context(tc.psum_pool(name="m_psum", bufs=M_BANKS))
        ctx.enter_context(tc.manual_schedule())

        warm = keep.tile([P, 2 * N], BF16, name="warm")
        warm_log = keep.tile([P, 1], F32, name="warm_log")
        nc.vector.memset(warm[:], 1.0)
        nc.scalar.activation(out=warm_log[:], in_=warm[:, 0:1], func=ACT.Ln)

        def warm_up(count):
            bank = m_psum.tile([P, 2, N], F32, name="m_bank")
            for i in range(count):
                nc.tensor.matmul(
                    out=bank[:].rearrange("p c n -> p (c n)"), lhsT=warm[:, :P], rhs=warm[:], start=True, stop=True
                )

        warm_up(WARM_FIRST)

        ident = keep.tile([P, P], F32, name="ident")
        make_identity(nc, ident[:])
        w_raw = keep.tile([P, TILES, K], BF16, name="w_raw")
        w_kt = keep.tile([P, TILES * WORDS], F32, name="w_kt", align_bytes=64)
        w_codes = keep.tile([P, 2 * N], U32, name="w_codes", align_bytes=64)
        w_scales = keep.tile([P, 2 * N], U8, name="w_scales", align_bytes=64)

        raw, t_banks, kt, codes, scales, m_banks, sq, held, power = {}, {}, {}, {}, {}, {}, {}, {}, {}

        def group_rows(g):
            return slice(first_pair[g] * PAIR * P, first_pair[g + 1] * PAIR * P)

        def load(g):
            n = SIZES[g] * PAIR
            raw[g] = raw_pool.tile([P, TILES, K], BF16, name="x_raw")
            nc.sync.dma_start(out=raw[g][:, :n, :], in_=x[group_rows(g), :].rearrange("(p j) k -> p j k", j=n))

        def transpose(src, i):
            words = src[:].rearrange("p j k -> p (j k)").bitcast(F32)
            bank = t_psum.tile([P, PAIR, 2, P], F32, name="t_bank")
            for jj in range(PAIR):
                w0 = (PAIR * i + jj) * WORDS
                for u in range(2):
                    nc.tensor.transpose(bank[:, jj, u, :], words[:, w0 + u : w0 + WORDS : 2], ident[:])
            return bank

        def interleave(copy, words, i, bank):
            width = PAIR * WORDS
            dst = words[:, i * width : (i + 1) * width].rearrange("p (j r u) -> p j r u", j=PAIR, u=2)
            copy(out=dst, in_=bank[:].rearrange("p j u r -> p j r u"))

        def transpose_x(q):
            g = group_of[q]
            t_banks[q] = transpose(raw[g], q - first_pair[g])

        def interleave_x(copy, q):
            g = group_of[q]
            if q == first_pair[g]:
                kt[g] = kt_pool.tile([P, VECTOR_ADD_COLS + TILES * WORDS], F32, name="kt", align_bytes=64)
            interleave(copy, kt[g][:, VECTOR_ADD_COLS:], q - first_pair[g], t_banks[q])

        def quantize_weights(half):
            cols = slice(half * N, (half + 1) * N)
            width = PAIR * WORDS
            nc.vector.quantize_mx(
                out=w_codes[:, cols].bitcast(E4M3X4),
                scales=w_scales[:, cols],
                in_=w_kt[:, half * width : (half + 1) * width].bitcast(BF16),
            )

        def quantize(g):
            n = SIZES[g] * PAIR
            codes[g] = code_pool.tile([P, TILES * P], U32, name="x_codes", align_bytes=64)
            scales[g] = code_pool.tile([P, TILES * P], U8, name="x_scales", align_bytes=64)
            nc.vector.quantize_mx(
                out=codes[g][:, : n * P].bitcast(E5M2X4),
                scales=scales[g][:, : n * P],
                in_=kt[g][:, VECTOR_ADD_COLS : VECTOR_ADD_COLS + n * WORDS].bitcast(BF16),
            )

        def tile_in_group(q, jj):
            return (q - first_pair[group_of[q]]) * PAIR + jj

        def multiply(q):
            g = group_of[q]
            for jj in range(PAIR):
                j = tile_in_group(q, jj)
                cols = slice(j * P, (j + 1) * P)
                bank = m_psum.tile([P, 2, N], F32, name="m_bank")
                nc.tensor.matmul_mx(
                    out=bank[:].rearrange("p c n -> p (c n)"),
                    lhsT=codes[g][:, cols].bitcast(E5M2X4),
                    lhsT_scale=scales[g][:, cols],
                    rhs=w_codes[:].bitcast(E4M3X4),
                    rhs_scale=w_scales[:],
                    start=True,
                    stop=True,
                )
                m_banks[q, jj] = bank

        def square_bank(q, jj, c0):
            j = tile_in_group(q, jj)
            nc.scalar.activation(out=sq[group_of[q]][:, :, j, c0:], in_=m_banks[q, jj][:, :, c0:], func=ACT.Square)

        def square_on_scalar(q):
            g = group_of[q]
            if q == first_pair[g]:
                sq[g] = sq_pool.tile([P, 2, TILES, N], F32, name="sq")
            for jj in range(PAIR):
                if jj > 0 or not vector_cols(q):
                    square_bank(q, jj, 0)
            if q + 1 < PAIRS and 0 < vector_cols(q + 1) < N:
                square_bank(q + 1, 0, vector_cols(q + 1))

        def hold(q):
            c0 = vector_cols(q)
            held[q] = held_pool.tile([P, 2, N], F32, name="held")
            nc.vector.tensor_copy(out=held[q][:, :, :c0], in_=m_banks[q, 0][:, :, :c0])

        def square_on_vector(q):
            c0 = vector_cols(q)
            nc.vector.tensor_tensor(
                out=sq[group_of[q]][:, :, tile_in_group(q, 0), :c0],
                in0=m_banks[q, 0][:, :, :c0],
                in1=held[q][:, :, :c0],
                op=ALU.mult,
            )

        def squares(g, part):
            return sq[g][:, part, :, :].rearrange("p j n -> p (j n)")

        def add_on(engine, g, cols):
            engine.tensor_tensor(
                out=power[g][:, cols], in0=squares(g, 0)[:, cols], in1=squares(g, 1)[:, cols], op=ALU.add
            )

        def add(g, s):
            width = SIZES[g] * PAIR * N
            v_cols = VECTOR_ADD_COLS if g >= SHORT_GROUPS else 0
            start = VECTOR_ADD_COLS - v_cols
            power[g] = kt[s][:, start : start + width]
            if v_cols:
                add_on(nc.vector, g, slice(0, v_cols))
            add_on(nc.gpsimd, g, slice(v_cols, width))

        def log_and_store(g, tiles):
            cols = slice(tiles.start * N, tiles.stop * N)
            res = res_pool.tile([P, TILES * N], F32, name="res")
            nc.scalar.activation(out=res[:, cols], in_=power[g][:, cols], func=ACT.Ln)
            rows = out[group_rows(g), :].rearrange("(p j) n -> p (j n)", j=SIZES[g] * PAIR)
            nc.sync.dma_start(out=rows[:, cols], in_=res[:, cols])

        nc.sync.dma_start(out=w_raw[:, :PAIR, :], in_=dft_real.rearrange("(j p) k -> p j k", p=P))
        nc.sync.dma_start(out=w_raw[:, PAIR:, :], in_=dft_imag.rearrange("(j p) k -> p j k", p=P))
        for g in range(LOAD_AHEAD):
            load(g)
        interleave(nc.scalar.copy, w_kt, 0, transpose(w_raw, 0))
        interleave(nc.vector.tensor_copy, w_kt, 1, transpose(w_raw, 1))
        warm_up(WARM_SECOND)
        transpose_x(0)
        interleave_x(nc.scalar.copy, 0)
        quantize_weights(0)
        quantize_weights(1)
        transpose_x(1)

        for s in range(GROUPS):
            if s + LOAD_AHEAD < GROUPS:
                load(s + LOAD_AHEAD)
            quantize(s)
            for g in range(s):
                if sum_step(g) == s:
                    add(g, s)
            for g in range(s):
                if sum_step(g) + 1 == s:
                    log_and_store(g, range(SIZES[g] * PAIR))
            for i in range(SIZES[s + 1] if s + 1 < GROUPS else 0):
                q = first_pair[s + 1] + i
                m = first_pair[s] + i if i < SIZES[s] else None
                if s < SHORT_GROUPS and m is not None:
                    multiply(m)
                if q + 1 < PAIRS:
                    transpose_x(q + 1)
                if s >= SHORT_GROUPS:
                    multiply(m)
                interleave_x(nc.vector.tensor_copy, q)
                if m is None:
                    continue
                if m - 2 in held:
                    square_on_vector(m - 2)
                if m < SHORT_GROUPS:
                    square_on_scalar(m)
                elif m > SHORT_GROUPS:
                    square_on_scalar(m - 1)
                    if vector_cols(m - 1):
                        hold(m - 1)

        before, first, second = range(PAIRS - 3, PAIRS)
        multiply(first)
        square_on_scalar(before)
        hold(before)
        multiply(second)
        square_on_vector(before)
        square_on_scalar(first)
        hold(first)
        square_on_vector(first)
        log_and_store(GROUPS - 3, range(TILES))
        square_on_scalar(second)
        for g in (GROUPS - 2, GROUPS - 1):
            power[g] = squares(g, 0)
            for j0 in range(0, TILES, PAIR):
                add_on(nc.vector, g, slice(j0 * N, (j0 + PAIR) * N))
                log_and_store(g, range(j0, j0 + PAIR))
